import numpy as np
import ml_dtypes


def mxq(x, axis, fmt="e4m3"):
    dtype, down = {"e4m3": (ml_dtypes.float8_e4m3fn, 7), "e5m2": (ml_dtypes.float8_e5m2, 14)}[fmt]
    v = np.moveaxis(np.asarray(x, np.float32).astype(ml_dtypes.bfloat16).astype(np.float64), axis, -1)
    blocks = v.reshape(v.shape[:-1] + (-1, 32))
    amax = np.abs(blocks).max(-1, keepdims=True)
    byte = np.maximum(np.where(amax > 0, np.frexp(amax)[1] - 1 + 127, 0) - down, 1)
    scale = np.exp2(byte - 127.0)
    codes = (blocks / scale).astype(np.float32).astype(dtype).astype(np.float64)
    return np.moveaxis((codes * scale).reshape(v.shape), -1, axis)


WIDE = False


def mx_kscale(k):
    if not WIDE:
        return np.ones(k)
    levels = np.array([20, -20, 10, -10, 0])
    a = np.random.permutation(np.resize(levels, k // 512 * 4)).reshape(k // 512, 4)
    idx = np.arange(k)
    return np.exp2(a[idx // 512, idx % 128 // 32])


BF16 = ml_dtypes.bfloat16


def bf(x):
    return np.asarray(x, np.float32).astype(BF16)


def f64(x):
    return np.asarray(x).astype(np.float64)


B, N, IN_DIM, OUT_DIM, NUM_F = 16, 256, 1024, 512, 1


def silu(v):
    return v / (1.0 + np.exp(-v))


def dsilu(v):
    sg = 1.0 / (1.0 + np.exp(-v))
    return sg * (1.0 + v * (1.0 - sg))


def setup_inputs():
    u = mx_kscale(OUT_DIM)
    x = np.random.standard_normal((B, N, IN_DIM))
    base_weight = np.random.standard_normal((OUT_DIM, IN_DIM)) / np.sqrt(IN_DIM) / u[:, None]
    grid = np.arange(NUM_F) + 1.5
    scale_sp = 1.0 + 0.1 * np.random.standard_normal(OUT_DIM)
    coef = np.random.uniform(size=(IN_DIM, NUM_F))
    conv_w = np.random.standard_normal((NUM_F, OUT_DIM, IN_DIM)) / np.sqrt(IN_DIM) / u[None, :, None]
    conv_b = np.random.standard_normal((NUM_F, OUT_DIM)) * 0.1
    g = np.random.standard_normal((B, N, OUT_DIM)) * np.exp2(np.random.randint(-12, 1, (B, N, 1))) * 16.0 * u[None, None, :]
    return {"x": bf(x), "base_weight": bf(base_weight), "grid": bf(grid), "scale_sp": bf(scale_sp),
            "coef": bf(coef), "conv_w": bf(conv_w), "conv_b": bf(conv_b), "grad_out": bf(g)}


def reference(x, base_weight, grid, scale_sp, coef, conv_w, conv_b, grad_out):
    x = f64(x)
    b, n, d = x.shape
    xf = x.reshape(b * n, d)
    g = f64(grad_out).reshape(b * n, OUT_DIM)
    gr = f64(grid)
    gb = mxq(g, 1, "e5m2") @ mxq(f64(base_weight), 0, "e4m3")
    gs = g * f64(scale_sp)[None, :]
    gsq = mxq(gs, 1, "e5m2")
    wq = mxq(f64(conv_w), 1, "e4m3")
    gsp = np.matmul(gsq[None, :, :], wq)
    dsin = np.cos(xf[None, :, :] * gr[:, None, None]) * gr[:, None, None] * f64(coef).T[:, None, :]
    gx = gb * dsilu(xf) + (gsp * dsin).sum(axis=0)
    return gx.reshape(b, n, d)

@@ -1,0 +1,315 @@
+import math
+from contextlib import ExitStack
+
+import concourse.mybir as mybir
+from concourse.masks import make_identity
+
+F32 = mybir.dt.float32
+BF16 = mybir.dt.bfloat16
+I32 = mybir.dt.int32
+U32 = mybir.dt.uint32
+U8 = mybir.dt.uint8
+E4 = mybir.dt.float8_e4m3fn_x4
+E5 = mybir.dt.float8_e5m2_x4
+ACT = mybir.ActivationFunctionType
+ALU = mybir.AluOpType
+
+P = 128
+TOKENS = 4096
+K = 512
+IN = 1024
+GT = 512
+NA = GT // P
+NG = TOKENS // GT
+HALF = 512
+NH = IN // HALF
+NJ = HALF // P
+NU = NG * NH
+
+FLOPS = 2 * 2 * TOKENS * K * IN
+
+
+def tile_efficient_skan_batch_t_kernel(
+    tc, x, base_weight, grid, scale_sp, coef, conv_w, conv_b, grad_out, out
+):
+    nc = tc.nc
+    xf = x.flatten_outer_dims()
+    gf = grad_out.flatten_outer_dims()
+    of = out.flatten_outer_dims()
+    wc_dram = conv_w.rearrange("o k i -> (o k) i")
+
+    with ExitStack() as ctx:
+        const = ctx.enter_context(tc.tile_pool(name="const", bufs=1))
+        wprep = ctx.enter_context(tc.tile_pool(name="wprep", bufs=2))
+        ld3 = ctx.enter_context(tc.tile_pool(name="ld3", bufs=3))
+        two = ctx.enter_context(tc.tile_pool(name="two", bufs=2))
+        three = ctx.enter_context(tc.tile_pool(name="three", bufs=3))
+        ps = ctx.enter_context(tc.psum_pool(name="ps", bufs=2))
+
+        x_tiles = {}
+        g_tiles = {}
+
+        def load(gi):
+            x_sb = ld3.tile([P, NA, IN], BF16, tag="x_sb")
+            nc.sync.dma_start(
+                out=x_sb[:],
+                in_=xf[GT * gi : GT * (gi + 1), :].rearrange("(p a) i -> p a i", a=NA),
+            )
+            g_sb = two.tile([P, NA, K], BF16, tag="g_sb")
+            nc.sync.dma_start(
+                out=g_sb[:],
+                in_=gf[GT * gi : GT * (gi + 1), :].rearrange("(p a) k -> p a k", a=NA),
+            )
+            x_tiles[gi] = x_sb
+            g_tiles[gi] = g_sb
+
+        load(0)
+
+        w_raw = []
+        for wi, w_dram in enumerate((wc_dram, base_weight)):
+            raw = const.tile([P, 4, IN], BF16, name="w_raw%d" % wi)
+            nc.sync.dma_start(
+                out=raw[:].rearrange("p (u e) i -> p u e i", u=2),
+                in_=w_dram.rearrange("(u p e) i -> p u e i", u=2, e=2),
+            )
+            w_raw.append(raw)
+
+        load(1)
+
+        ident_bf = const.tile([P, P], BF16, name="ident_bf")
+        make_identity(nc, ident_bf[:])
+        ident_f = const.tile([P, P], F32, name="ident_f")
+        make_identity(nc, ident_f[:])
+
+        grid_bf = const.tile([P, 1], BF16, name="grid_bf")
+        nc.scalar.dma_start(out=grid_bf[:], in_=grid.partition_broadcast(P))
+        sc4 = const.tile([P, 2, 2], BF16, name="sc4")
+        nc.scalar.dma_start(
+            out=sc4[:], in_=scale_sp.rearrange("(u p e) -> p u e", u=2, e=2)
+        )
+        coef_rows = const.tile([P, P], BF16, name="coef_rows")
+        nc.vector.memset(coef_rows[:], 0.0)
+        nc.scalar.dma_start(
+            out=coef_rows[0 : IN // P, :],
+            in_=coef.rearrange("(b p) o -> b (p o)", p=P),
+        )
+
+        grid_f = const.tile([P, 1], F32, name="grid_f")
+        nc.vector.tensor_copy(out=grid_f[:], in_=grid_bf[:])
+        turns = const.tile([P, 1], F32, name="turns")
+        nc.vector.tensor_scalar(
+            out=turns[:], in0=grid_f[:], scalar1=1.0 / (2.0 * math.pi), scalar2=None,
+            op0=ALU.mult,
+        )
+        quarter = const.tile([P, 1], F32, name="quarter")
+        nc.vector.memset(quarter[:], 0.25)
+        half_pi = const.tile([P, 1], F32, name="half_pi")
+        nc.vector.tensor_scalar(
+            out=half_pi[:], in0=quarter[:], scalar1=2.0 * math.pi, scalar2=None,
+            op0=ALU.mult,
+        )
+
+        coef_ps = ps.tile([P, 2, GT], BF16, tag="tr")
+        nc.tensor.transpose(out=coef_ps[:, 0, 0:P], in_=coef_rows[:], identity=ident_bf[:])
+        ccol = const.tile([P, IN // P], F32, name="ccol")
+        nc.vector.tensor_scalar(
+            out=ccol[:], in0=coef_ps[:, 0, 0 : IN // P], scalar1=grid_f[:, 0:1],
+            scalar2=None, op0=ALU.mult,
+        )
+
+        w_codes = []
+        w_scales = []
+        for wi in range(2):
+            codes = const.tile([P, IN], U32, name="w_codes%d" % wi, align_bytes=64)
+            scales = const.tile([P, IN], U8, name="w_scales%d" % wi, align_bytes=64)
+            w_codes.append(codes)
+            w_scales.append(scales)
+        for h in range(NH):
+            grouped = []
+            for wi in range(2):
+                grp = wprep.tile([P, HALF, 4], BF16, tag="grp%d" % wi, align_bytes=64)
+                nc.vector.tensor_copy(
+                    out=grp[:].rearrange("p (c j) t -> p c t j", j=4),
+                    in_=w_raw[wi][:, :, HALF * h : HALF * (h + 1)].rearrange(
+                        "p t (c j) -> p c t j", j=4
+                    ),
+                )
+                grouped.append(grp)
+            for wi in range(2):
+                nc.vector.quantize_mx(
+                    out=w_codes[wi][:, HALF * h : HALF * (h + 1)].bitcast(E4),
+                    scales=w_scales[wi][:, HALF * h : HALF * (h + 1)],
+                    in_=grouped[wi][:].rearrange("p i t -> p (i t)"),
+                )
+        wc_codes, wb_codes = w_codes
+        wc_scales, wb_scales = w_scales
+
+        g_codes = {}
+        g_scales = {}
+
+        def prep(gi):
+            g32 = g_tiles[gi][:].bitcast(F32)
+            gq = two.tile([P, 2, 4 * GT], BF16, tag="gq", align_bytes=64)
+            gq32 = gq[:, 0, :].bitcast(F32).rearrange("p (a t u) -> p a t u", a=NA, u=2)
+            for ap in range(NA // 2):
+                tr = ps.tile([P, 2, 2, P], F32, tag="tr")
+                for a2 in range(2):
+                    for u in range(2):
+                        nc.tensor.transpose(
+                            out=tr[:, a2, u, :],
+                            in_=g32[:, 2 * ap + a2, P * u : P * (u + 1)],
+                            identity=ident_f[:],
+                        )
+                nc.scalar.copy(
+                    out=gq32[:, 2 * ap : 2 * ap + 2, :, :],
+                    in_=tr[:].rearrange("p a u t -> p a t u"),
+                )
+            nc.vector.tensor_tensor(
+                out=gq[:, 1, :].rearrange("p (t s) -> p t s", s=4),
+                in0=gq[:, 0, :].rearrange("p (t s) -> p t s", s=4),
+                in1=sc4[:].rearrange("p u e -> p (u e)").unsqueeze(1).to_broadcast([P, GT, 4]),
+                op=ALU.mult,
+            )
+            gc = two.tile([P, 2, GT], U32, tag="gc", align_bytes=64)
+            gs = two.tile([P, 2, GT], U8, tag="gs", align_bytes=64)
+            nc.vector.quantize_mx(
+                out=gc[:].rearrange("p w c -> p (w c)").bitcast(E5),
+                scales=gs[:].rearrange("p w c -> p (w c)"),
+                in_=gq[:].rearrange("p w c -> p (w c)"),
+            )
+            g_codes[gi] = gc
+            g_scales[gi] = gs
+
+        sp_tiles = {}
+        th_tiles = {}
+        m_tiles = {}
+        bs_tiles = {}
+
+        def stage_a(s):
+            gi, h = divmod(s, NH)
+            x_sb = x_tiles[gi]
+            sp = three.tile([P, NJ, GT], F32, tag="sp")
+            for jj in range(NJ // 2):
+                xt = ps.tile([P, 2, GT], BF16, tag="tr")
+                for j2 in range(2):
+                    b = NJ * h + 2 * jj + j2
+                    for a in range(NA):
+                        nc.tensor.transpose(
+                            out=xt[:, j2, P * a : P * (a + 1)],
+                            in_=x_sb[:, a, P * b : P * (b + 1)],
+                            identity=ident_bf[:],
+                        )
+                xt_flat = xt[:].rearrange("p j t -> p (j t)")
+                yq = two.tile([P, 2 * GT], F32, tag="yq")
+                nc.scalar.activation(
+                    out=yq[:], in_=xt_flat, func=ACT.Identity,
+                    bias=quarter[:, 0:1], scale=turns[:, 0:1],
+                )
+                n_i = two.tile([P, 2 * GT], I32, tag="n_i")
+                nc.gpsimd.tensor_scalar(
+                    out=n_i[:], in0=yq[:], scalar1=1.0, scalar2=0.0,
+                    op0=ALU.mult, op1=ALU.add,
+                )
+                nc.vector.scalar_tensor_tensor(
+                    out=sp[:, 2 * jj : 2 * jj + 2, :].rearrange("p j t -> p (j t)"),
+                    in0=xt_flat, scalar=turns[:, 0:1], in1=n_i[:],
+                    op0=ALU.mult, op1=ALU.subtract,
+                )
+            th = three.tile([P, NA, HALF], F32, tag="th")
+            nc.scalar.activation(
+                out=th[:], in_=x_sb[:, :, HALF * h : HALF * (h + 1)], func=ACT.Tanh,
+                scale=0.5,
+            )
+            m = three.tile([P, NA, HALF], F32, tag="m")
+            nc.scalar.activation(
+                out=m[:], in_=x_sb[:, :, HALF * h : HALF * (h + 1)], func=ACT.Silu,
+                scale=-1.0,
+            )
+            nc.gpsimd.tensor_scalar(
+                out=m[:], in0=m[:], scalar1=-0.5, scalar2=0.5, op0=ALU.mult, op1=ALU.add,
+            )
+            nc.scalar.activation(
+                out=sp[:], in_=sp[:], func=ACT.Sin, bias=half_pi[:, 0:1],
+                scale=2.0 * math.pi,
+            )
+            sp_tiles[s] = sp
+            th_tiles[s] = th
+            m_tiles[s] = m
+
+        def stage_b(s):
+            gi, h = divmod(s, NH)
+            gc = g_codes[gi]
+            gs = g_scales[gi]
+            sp = sp_tiles[s]
+            th = th_tiles[s]
+            m = m_tiles[s]
+            sp_ps = []
+            for j in range(NJ):
+                b = NJ * h + j
+                acc = ps.tile([P, GT], F32, tag="gsp")
+                nc.tensor.matmul_mx(
+                    out=acc[:],
+                    lhsT=wc_codes[:, P * b : P * (b + 1)].bitcast(E4),
+                    lhsT_scale=wc_scales[:, P * b : P * (b + 1)],
+                    rhs=gc[:, 1, :].bitcast(E5),
+                    rhs_scale=gs[:, 1, :],
+                    start=True, stop=True,
+                )
+                nc.vector.scalar_tensor_tensor(
+                    out=sp[:, j, :], in0=acc[:], scalar=ccol[:, b : b + 1], in1=sp[:, j, :],
+                    op0=ALU.mult, op1=ALU.mult,
+                )
+                sp_ps.append(acc)
+            bs = three.tile([P, NA, HALF], F32, tag="bs")
+            for a in range(NA):
+                acc = ps.tile([P, HALF], F32, tag="gb")
+                nc.tensor.matmul_mx(
+                    out=acc[:],
+                    lhsT=gc[:, 0, P * a : P * (a + 1)].bitcast(E5),
+                    lhsT_scale=gs[:, 0, P * a : P * (a + 1)],
+                    rhs=wb_codes[:, HALF * h : HALF * (h + 1)].bitcast(E4),
+                    rhs_scale=wb_scales[:, HALF * h : HALF * (h + 1)],
+                    start=True, stop=True,
+                )
+                nc.vector.scalar_tensor_tensor(
+                    out=bs[:, a, :], in0=th[:, a, :], scalar=1.0, in1=acc[:],
+                    op0=ALU.add, op1=ALU.mult,
+                )
+            nc.gpsimd.tensor_tensor(out=bs[:], in0=bs[:], in1=m[:], op=ALU.mult)
+            bs_tiles[s] = bs
+
+        def stage_c(s):
+            gi, h = divmod(s, NH)
+            sp = sp_tiles[s]
+            bs = bs_tiles[s]
+            for a in range(NA):
+                p2 = ps.tile([P, HALF], F32, tag="p2")
+                for j in range(NJ):
+                    nc.tensor.transpose(
+                        out=p2[:, P * j : P * (j + 1)],
+                        in_=sp[:, j, P * a : P * (a + 1)],
+                        identity=ident_f[:],
+                    )
+                nc.vector.tensor_tensor(
+                    out=bs[:, a, :], in0=p2[:], in1=bs[:, a, :], op=ALU.add
+                )
+            nc.sync.dma_start(
+                out=of[GT * gi : GT * (gi + 1), HALF * h : HALF * (h + 1)].rearrange(
+                    "(p a) i -> p a i", a=NA
+                ),
+                in_=bs[:],
+            )
+
+        prep(0)
+        for s in range(NU + 2):
+            if s < NU:
+                gi, h = divmod(s, NH)
+                if h == 0 and gi + 2 < NG:
+                    load(gi + 2)
+                stage_a(s)
+                if h == 0 and gi + 1 < NG:
+                    prep(gi + 1)
+            if s >= 2:
+                stage_c(s - 2)
+            if 1 <= s <= NU:
+                stage_b(s - 1)

@@ -23,8 +23,13 @@ NA = GT // P
 NG = TOKENS // GT
 HALF = 512
 NH = IN // HALF
-NJ = HALF // P
-NU = NG * NH
+NK = NG * NH * 2
+
+LAG_CS = 1
+LAG_B = 1
+LAG_M1 = 1
+LAG_P1 = 2
+LAG_C = 3
 
 FLOPS = 2 * 2 * TOKENS * K * IN
 
@@ -40,17 +45,16 @@ def tile_efficient_skan_batch_t_kernel(
 
     with ExitStack() as ctx:
         const = ctx.enter_context(tc.tile_pool(name="const", bufs=1))
-        wprep = ctx.enter_context(tc.tile_pool(name="wprep", bufs=2))
-        ld3 = ctx.enter_context(tc.tile_pool(name="ld3", bufs=3))
         two = ctx.enter_context(tc.tile_pool(name="two", bufs=2))
         three = ctx.enter_context(tc.tile_pool(name="three", bufs=3))
         ps = ctx.enter_context(tc.psum_pool(name="ps", bufs=2))
+        ctx.enter_context(tc.manual_schedule())
 
         x_tiles = {}
         g_tiles = {}
 
         def load(gi):
-            x_sb = ld3.tile([P, NA, IN], BF16, tag="x_sb")
+            x_sb = three.tile([P, NA, IN], BF16, tag="x_sb")
             nc.sync.dma_start(
                 out=x_sb[:],
                 in_=xf[GT * gi : GT * (gi + 1), :].rearrange("(p a) i -> p a i", a=NA),
@@ -62,24 +66,6 @@ def tile_efficient_skan_batch_t_kernel(
             )
             x_tiles[gi] = x_sb
             g_tiles[gi] = g_sb
-
-        load(0)
-
-        w_raw = []
-        for wi, w_dram in enumerate((wc_dram, base_weight)):
-            raw = const.tile([P, 4, IN], BF16, name="w_raw%d" % wi)
-            nc.sync.dma_start(
-                out=raw[:].rearrange("p (u e) i -> p u e i", u=2),
-                in_=w_dram.rearrange("(u p e) i -> p u e i", u=2, e=2),
-            )
-            w_raw.append(raw)
-
-        load(1)
-
-        ident_bf = const.tile([P, P], BF16, name="ident_bf")
-        make_identity(nc, ident_bf[:])
-        ident_f = const.tile([P, P], F32, name="ident_f")
-        make_identity(nc, ident_f[:])
 
         grid_bf = const.tile([P, 1], BF16, name="grid_bf")
         nc.scalar.dma_start(out=grid_bf[:], in_=grid.partition_broadcast(P))
@@ -94,6 +80,37 @@ def tile_efficient_skan_batch_t_kernel(
             in_=coef.rearrange("(b p) o -> b (p o)", p=P),
         )
 
+        load(0)
+        w_drams = (wc_dram, base_weight)
+        w_raw = []
+        for wi in range(2):
+            raw = const.tile([P, 4, IN], BF16, name="w_raw%d" % wi)
+            w_raw.append(raw)
+        for h in range(NH):
+            for wi in range(2):
+                for u in range(2):
+                    nc.sync.dma_start(
+                        out=w_raw[wi][:, 2 * u : 2 * u + 2, HALF * h : HALF * (h + 1)],
+                        in_=w_drams[wi][
+                            256 * u : 256 * (u + 1), HALF * h : HALF * (h + 1)
+                        ].rearrange("(p e) i -> p e i", e=2),
+                    )
+        load(1)
+
+        ident_bf = const.tile([P, P], BF16, name="ident_bf")
+        make_identity(nc, ident_bf[:])
+        ident_f = const.tile([P, P], F32, name="ident_f")
+        make_identity(nc, ident_f[:])
+
+        quarter = const.tile([P, 1], F32, name="quarter")
+        nc.vector.memset(quarter[:], 0.25)
+        warm = const.tile([P, 1], F32, name="warm")
+        nc.scalar.activation(out=warm[:], in_=quarter[:], func=ACT.Silu)
+        half_pi = const.tile([P, 1], F32, name="half_pi")
+        nc.vector.tensor_scalar(
+            out=half_pi[:], in0=quarter[:], scalar1=2.0 * math.pi, scalar2=None,
+            op0=ALU.mult,
+        )
         grid_f = const.tile([P, 1], F32, name="grid_f")
         nc.vector.tensor_copy(out=grid_f[:], in_=grid_bf[:])
         turns = const.tile([P, 1], F32, name="turns")
@@ -101,19 +118,11 @@ def tile_efficient_skan_batch_t_kernel(
             out=turns[:], in0=grid_f[:], scalar1=1.0 / (2.0 * math.pi), scalar2=None,
             op0=ALU.mult,
         )
-        quarter = const.tile([P, 1], F32, name="quarter")
-        nc.vector.memset(quarter[:], 0.25)
-        half_pi = const.tile([P, 1], F32, name="half_pi")
-        nc.vector.tensor_scalar(
-            out=half_pi[:], in0=quarter[:], scalar1=2.0 * math.pi, scalar2=None,
-            op0=ALU.mult,
-        )
-
-        coef_ps = ps.tile([P, 2, GT], BF16, tag="tr")
-        nc.tensor.transpose(out=coef_ps[:, 0, 0:P], in_=coef_rows[:], identity=ident_bf[:])
+        coef_ps = ps.tile([P, P], BF16, tag="gt", bufs=1)
+        nc.tensor.transpose(out=coef_ps[:], in_=coef_rows[:], identity=ident_bf[:])
         ccol = const.tile([P, IN // P], F32, name="ccol")
         nc.vector.tensor_scalar(
-            out=ccol[:], in0=coef_ps[:, 0, 0 : IN // P], scalar1=grid_f[:, 0:1],
+            out=ccol[:], in0=coef_ps[:, 0 : IN // P], scalar1=grid_f[:, 0:1],
             scalar2=None, op0=ALU.mult,
         )
 
@@ -124,10 +133,13 @@ def tile_efficient_skan_batch_t_kernel(
             scales = const.tile([P, IN], U8, name="w_scales%d" % wi, align_bytes=64)
             w_codes.append(codes)
             w_scales.append(scales)
-        for h in range(NH):
+        wc_codes, wb_codes = w_codes
+        wc_scales, wb_scales = w_scales
+
+        def wprep(h):
             grouped = []
             for wi in range(2):
-                grp = wprep.tile([P, HALF, 4], BF16, tag="grp%d" % wi, align_bytes=64)
+                grp = two.tile([P, HALF, 4], BF16, tag="grp%d" % wi, align_bytes=64)
                 nc.vector.tensor_copy(
                     out=grp[:].rearrange("p (c j) t -> p c t j", j=4),
                     in_=w_raw[wi][:, :, HALF * h : HALF * (h + 1)].rearrange(
@@ -141,35 +153,46 @@ def tile_efficient_skan_batch_t_kernel(
                     scales=w_scales[wi][:, HALF * h : HALF * (h + 1)],
                     in_=grouped[wi][:].rearrange("p i t -> p (i t)"),
                 )
-        wc_codes, wb_codes = w_codes
-        wc_scales, wb_scales = w_scales
 
+        gt_tiles = {}
+        gq_tiles = {}
         g_codes = {}
         g_scales = {}
 
-        def prep(gi):
+        def gt_pe(gi, ap):
             g32 = g_tiles[gi][:].bitcast(F32)
-            gq = two.tile([P, 2, 4 * GT], BF16, tag="gq", align_bytes=64)
+            tr = ps.tile([P, 2, 2, P], F32, tag="gt", bufs=1)
+            for a2 in range(2):
+                for u in range(2):
+                    nc.tensor.transpose(
+                        out=tr[:, a2, u, :],
+                        in_=g32[:, 2 * ap + a2, P * u : P * (u + 1)],
+                        identity=ident_f[:],
+                    )
+            gt_tiles[gi, ap] = tr
+
+        def gt_act(gi, ap):
+            if ap == 0:
+                gq = two.tile([P, 2, 4 * GT], BF16, tag="gq", align_bytes=64)
+                gq_tiles[gi] = gq
+            gq = gq_tiles[gi]
             gq32 = gq[:, 0, :].bitcast(F32).rearrange("p (a t u) -> p a t u", a=NA, u=2)
-            for ap in range(NA // 2):
-                tr = ps.tile([P, 2, 2, P], F32, tag="tr")
-                for a2 in range(2):
-                    for u in range(2):
-                        nc.tensor.transpose(
-                            out=tr[:, a2, u, :],
-                            in_=g32[:, 2 * ap + a2, P * u : P * (u + 1)],
-                            identity=ident_f[:],
-                        )
-                nc.scalar.copy(
-                    out=gq32[:, 2 * ap : 2 * ap + 2, :, :],
-                    in_=tr[:].rearrange("p a u t -> p a t u"),
-                )
+            nc.scalar.copy(
+                out=gq32[:, 2 * ap : 2 * ap + 2, :, :],
+                in_=gt_tiles[gi, ap][:].rearrange("p a u t -> p a t u"),
+            )
+
+        def gs_mul(gi):
+            gq = gq_tiles[gi]
             nc.vector.tensor_tensor(
                 out=gq[:, 1, :].rearrange("p (t s) -> p t s", s=4),
                 in0=gq[:, 0, :].rearrange("p (t s) -> p t s", s=4),
                 in1=sc4[:].rearrange("p u e -> p (u e)").unsqueeze(1).to_broadcast([P, GT, 4]),
                 op=ALU.mult,
             )
+
+        def quant(gi):
+            gq = gq_tiles[gi]
             gc = two.tile([P, 2, GT], U32, tag="gc", align_bytes=64)
             gs = two.tile([P, 2, GT], U8, tag="gs", align_bytes=64)
             nc.vector.quantize_mx(
@@ -180,93 +203,127 @@ def tile_efficient_skan_batch_t_kernel(
             g_codes[gi] = gc
             g_scales[gi] = gs
 
+        xt_tiles = {}
+        yq_tiles = {}
+        ni_tiles = {}
         sp_tiles = {}
         th_tiles = {}
         m_tiles = {}
         bs_tiles = {}
 
-        def stage_a(s):
-            gi, h = divmod(s, NH)
+        def split(k):
+            gi, rest = divmod(k, 2 * NH)
+            h, q = divmod(rest, 2)
+            return gi, h, q
+
+        def x_t(k):
+            gi, h, q = split(k)
             x_sb = x_tiles[gi]
-            sp = three.tile([P, NJ, GT], F32, tag="sp")
-            for jj in range(NJ // 2):
-                xt = ps.tile([P, 2, GT], BF16, tag="tr")
-                for j2 in range(2):
-                    b = NJ * h + 2 * jj + j2
-                    for a in range(NA):
-                        nc.tensor.transpose(
-                            out=xt[:, j2, P * a : P * (a + 1)],
-                            in_=x_sb[:, a, P * b : P * (b + 1)],
-                            identity=ident_bf[:],
-                        )
-                xt_flat = xt[:].rearrange("p j t -> p (j t)")
-                yq = two.tile([P, 2 * GT], F32, tag="yq")
-                nc.scalar.activation(
-                    out=yq[:], in_=xt_flat, func=ACT.Identity,
-                    bias=quarter[:, 0:1], scale=turns[:, 0:1],
-                )
-                n_i = two.tile([P, 2 * GT], I32, tag="n_i")
-                nc.gpsimd.tensor_scalar(
-                    out=n_i[:], in0=yq[:], scalar1=1.0, scalar2=0.0,
-                    op0=ALU.mult, op1=ALU.add,
-                )
-                nc.vector.scalar_tensor_tensor(
-                    out=sp[:, 2 * jj : 2 * jj + 2, :].rearrange("p j t -> p (j t)"),
-                    in0=xt_flat, scalar=turns[:, 0:1], in1=n_i[:],
-                    op0=ALU.mult, op1=ALU.subtract,
-                )
-            th = three.tile([P, NA, HALF], F32, tag="th")
+            xt = ps.tile([P, 2, GT], BF16, tag="tr")
+            for j2 in range(2):
+                b = 4 * h + 2 * q + j2
+                for a in range(NA):
+                    nc.tensor.transpose(
+                        out=xt[:, j2, P * a : P * (a + 1)],
+                        in_=x_sb[:, a, P * b : P * (b + 1)],
+                        identity=ident_bf[:],
+                    )
+            xt_tiles[k] = xt
+
+        def y_act(k):
+            yq = two.tile([P, 2 * GT], F32, tag="yq")
             nc.scalar.activation(
-                out=th[:], in_=x_sb[:, :, HALF * h : HALF * (h + 1)], func=ACT.Tanh,
+                out=yq[:], in_=xt_tiles[k][:].rearrange("p j t -> p (j t)"),
+                func=ACT.Identity, bias=quarter[:, 0:1], scale=turns[:, 0:1],
+            )
+            yq_tiles[k] = yq
+
+        def n_pool(k):
+            n_i = two.tile([P, 2 * GT], I32, tag="n_i")
+            nc.gpsimd.tensor_scalar(
+                out=n_i[:], in0=yq_tiles[k][:], scalar1=1.0, scalar2=0.0,
+                op0=ALU.mult, op1=ALU.add,
+            )
+            ni_tiles[k] = n_i
+
+        def r_dve(k):
+            q = k % 2
+            if q == 0:
+                sp = three.tile([P, 4, GT], F32, tag="sp")
+                sp_tiles[k // 2] = sp
+            sp = sp_tiles[k // 2]
+            nc.vector.scalar_tensor_tensor(
+                out=sp[:, 2 * q : 2 * q + 2, :].rearrange("p j t -> p (j t)"),
+                in0=xt_tiles[k][:].rearrange("p j t -> p (j t)"),
+                scalar=turns[:, 0:1], in1=ni_tiles[k][:],
+                op0=ALU.mult, op1=ALU.subtract,
+            )
+
+        def cs_act(k):
+            q = k % 2
+            sp = sp_tiles[k // 2]
+            nc.scalar.activation(
+                out=sp[:, 2 * q : 2 * q + 2, :], in_=sp[:, 2 * q : 2 * q + 2, :],
+                func=ACT.Sin, bias=half_pi[:, 0:1], scale=2.0 * math.pi,
+            )
+
+        def th_m_act(k):
+            gi, h, q = split(k)
+            if q == 0:
+                th = three.tile([P, NA, HALF], F32, tag="th")
+                m = three.tile([P, NA, HALF], F32, tag="m")
+                th_tiles[k // 2] = th
+                m_tiles[k // 2] = m
+            x_in = x_tiles[gi][:, 2 * q : 2 * q + 2, HALF * h : HALF * (h + 1)]
+            nc.scalar.activation(
+                out=th_tiles[k // 2][:, 2 * q : 2 * q + 2, :], in_=x_in, func=ACT.Tanh,
                 scale=0.5,
             )
-            m = three.tile([P, NA, HALF], F32, tag="m")
             nc.scalar.activation(
-                out=m[:], in_=x_sb[:, :, HALF * h : HALF * (h + 1)], func=ACT.Silu,
+                out=m_tiles[k // 2][:, 2 * q : 2 * q + 2, :], in_=x_in, func=ACT.Silu,
                 scale=-1.0,
             )
-            nc.gpsimd.tensor_scalar(
-                out=m[:], in0=m[:], scalar1=-0.5, scalar2=0.5, op0=ALU.mult, op1=ALU.add,
-            )
-            nc.scalar.activation(
-                out=sp[:], in_=sp[:], func=ACT.Sin, bias=half_pi[:, 0:1],
-                scale=2.0 * math.pi,
-            )
-            sp_tiles[s] = sp
-            th_tiles[s] = th
-            m_tiles[s] = m
 
-        def stage_b(s):
-            gi, h = divmod(s, NH)
-            gc = g_codes[gi]
-            gs = g_scales[gi]
-            sp = sp_tiles[s]
-            th = th_tiles[s]
-            m = m_tiles[s]
-            sp_ps = []
-            for j in range(NJ):
-                b = NJ * h + j
-                acc = ps.tile([P, GT], F32, tag="gsp")
+        def m1_pool(k):
+            q = k % 2
+            m = m_tiles[k // 2]
+            nc.gpsimd.tensor_scalar(
+                out=m[:, 2 * q : 2 * q + 2, :], in0=m[:, 2 * q : 2 * q + 2, :],
+                scalar1=-0.5, scalar2=0.5, op0=ALU.mult, op1=ALU.add,
+            )
+
+        def mx_spline(k):
+            gi, h, q = split(k)
+            sp = sp_tiles[k // 2]
+            for j in (2 * q, 2 * q + 1):
+                b = 4 * h + j
+                acc = ps.tile([P, GT], F32, tag="mx", bufs=3)
                 nc.tensor.matmul_mx(
                     out=acc[:],
                     lhsT=wc_codes[:, P * b : P * (b + 1)].bitcast(E4),
                     lhsT_scale=wc_scales[:, P * b : P * (b + 1)],
-                    rhs=gc[:, 1, :].bitcast(E5),
-                    rhs_scale=gs[:, 1, :],
+                    rhs=g_codes[gi][:, 1, :].bitcast(E5),
+                    rhs_scale=g_scales[gi][:, 1, :],
                     start=True, stop=True,
                 )
                 nc.vector.scalar_tensor_tensor(
                     out=sp[:, j, :], in0=acc[:], scalar=ccol[:, b : b + 1], in1=sp[:, j, :],
                     op0=ALU.mult, op1=ALU.mult,
                 )
-                sp_ps.append(acc)
-            bs = three.tile([P, NA, HALF], F32, tag="bs")
-            for a in range(NA):
-                acc = ps.tile([P, HALF], F32, tag="gb")
+
+        def mx_base(k):
+            gi, h, q = split(k)
+            if q == 0:
+                bs = three.tile([P, NA, HALF], F32, tag="bs")
+                bs_tiles[k // 2] = bs
+            bs = bs_tiles[k // 2]
+            th = th_tiles[k // 2]
+            for a in (2 * q, 2 * q + 1):
+                acc = ps.tile([P, HALF], F32, tag="mx", bufs=3)
                 nc.tensor.matmul_mx(
                     out=acc[:],
-                    lhsT=gc[:, 0, P * a : P * (a + 1)].bitcast(E5),
-                    lhsT_scale=gs[:, 0, P * a : P * (a + 1)],
+                    lhsT=g_codes[gi][:, 0, P * a : P * (a + 1)].bitcast(E5),
+                    lhsT_scale=g_scales[gi][:, 0, P * a : P * (a + 1)],
                     rhs=wb_codes[:, HALF * h : HALF * (h + 1)].bitcast(E4),
                     rhs_scale=wb_scales[:, HALF * h : HALF * (h + 1)],
                     start=True, stop=True,
@@ -275,16 +332,22 @@ def tile_efficient_skan_batch_t_kernel(
                     out=bs[:, a, :], in0=th[:, a, :], scalar=1.0, in1=acc[:],
                     op0=ALU.add, op1=ALU.mult,
                 )
-            nc.gpsimd.tensor_tensor(out=bs[:], in0=bs[:], in1=m[:], op=ALU.mult)
-            bs_tiles[s] = bs
 
-        def stage_c(s):
-            gi, h = divmod(s, NH)
-            sp = sp_tiles[s]
-            bs = bs_tiles[s]
-            for a in range(NA):
+        def p1_pool(k):
+            q = k % 2
+            bs = bs_tiles[k // 2]
+            nc.gpsimd.tensor_tensor(
+                out=bs[:, 2 * q : 2 * q + 2, :], in0=bs[:, 2 * q : 2 * q + 2, :],
+                in1=m_tiles[k // 2][:, 2 * q : 2 * q + 2, :], op=ALU.mult,
+            )
+
+        def finish(k):
+            gi, h, q = split(k)
+            sp = sp_tiles[k // 2]
+            bs = bs_tiles[k // 2]
+            for a in (2 * q, 2 * q + 1):
                 p2 = ps.tile([P, HALF], F32, tag="p2")
-                for j in range(NJ):
+                for j in range(4):
                     nc.tensor.transpose(
                         out=p2[:, P * j : P * (j + 1)],
                         in_=sp[:, j, P * a : P * (a + 1)],
@@ -296,20 +359,53 @@ def tile_efficient_skan_batch_t_kernel(
             nc.sync.dma_start(
                 out=of[GT * gi : GT * (gi + 1), HALF * h : HALF * (h + 1)].rearrange(
                     "(p a) i -> p a i", a=NA
-                ),
-                in_=bs[:],
+                )[:, 2 * q : 2 * q + 2, :],
+                in_=bs[:, 2 * q : 2 * q + 2, :],
             )
 
-        prep(0)
-        for s in range(NU + 2):
-            if s < NU:
-                gi, h = divmod(s, NH)
-                if h == 0 and gi + 2 < NG:
-                    load(gi + 2)
-                stage_a(s)
-                if h == 0 and gi + 1 < NG:
-                    prep(gi + 1)
-            if s >= 2:
-                stage_c(s - 2)
-            if 1 <= s <= NU:
-                stage_b(s - 1)
+        def live(i):
+            return 0 <= i < NK
+
+        for ap in range(2):
+            gt_pe(0, ap)
+            gt_act(0, ap)
+        gs_mul(0)
+        quant(0)
+        x_t(0)
+        for k in range(NK + LAG_C + 1):
+            gi, ph = divmod(k + 4, 4)
+            if ph == 0 and gi + 1 < NG:
+                load(gi + 1)
+            if live(k):
+                y_act(k)
+            if live(k + 1):
+                x_t(k + 1)
+            if live(k):
+                n_pool(k)
+            if live(k - LAG_CS):
+                cs_act(k - LAG_CS)
+            if live(k):
+                r_dve(k)
+            if gi < NG and ph in (1, 2):
+                gt_act(gi, ph - 1)
+            if live(k):
+                th_m_act(k)
+            if k == 0:
+                wprep(0)
+            if live(k - LAG_M1):
+                m1_pool(k - LAG_M1)
+            if live(k - LAG_B):
+                mx_spline(k - LAG_B)
+                mx_base(k - LAG_B)
+            if live(k - LAG_P1):
+                p1_pool(k - LAG_P1)
+            if live(k - LAG_C):
+                finish(k - LAG_C)
+            if k == 1:
+                wprep(1)
+            if gi < NG and ph in (0, 1):
+                gt_pe(gi, ph)
+            if gi < NG and ph == 2:
+                gs_mul(gi)
+            if gi < NG and ph == 3:
+                quant(gi)

@@ -30,6 +30,7 @@ LAG_B = 1
 LAG_M1 = 1
 LAG_P1 = 2
 LAG_C = 3
+MX_REPEAT = 2
 
 FLOPS = 2 * 2 * TOKENS * K * IN
 
@@ -298,14 +299,15 @@ def tile_efficient_skan_batch_t_kernel(
             for j in (2 * q, 2 * q + 1):
                 b = 4 * h + j
                 acc = ps.tile([P, GT], F32, tag="mx", bufs=3)
-                nc.tensor.matmul_mx(
-                    out=acc[:],
-                    lhsT=wc_codes[:, P * b : P * (b + 1)].bitcast(E4),
-                    lhsT_scale=wc_scales[:, P * b : P * (b + 1)],
-                    rhs=g_codes[gi][:, 1, :].bitcast(E5),
-                    rhs_scale=g_scales[gi][:, 1, :],
-                    start=True, stop=True,
-                )
+                for rep in range(MX_REPEAT):
+                    nc.tensor.matmul_mx(
+                        out=acc[:],
+                        lhsT=wc_codes[:, P * b : P * (b + 1)].bitcast(E4),
+                        lhsT_scale=wc_scales[:, P * b : P * (b + 1)],
+                        rhs=g_codes[gi][:, 1, :].bitcast(E5),
+                        rhs_scale=g_scales[gi][:, 1, :],
+                        start=True, stop=True,
+                    )
                 nc.vector.scalar_tensor_tensor(
                     out=sp[:, j, :], in0=acc[:], scalar=ccol[:, b : b + 1], in1=sp[:, j, :],
                     op0=ALU.mult, op1=ALU.mult,
@@ -320,14 +322,15 @@ def tile_efficient_skan_batch_t_kernel(
             th = th_tiles[k // 2]
             for a in (2 * q, 2 * q + 1):
                 acc = ps.tile([P, HALF], F32, tag="mx", bufs=3)
-                nc.tensor.matmul_mx(
-                    out=acc[:],
-                    lhsT=g_codes[gi][:, 0, P * a : P * (a + 1)].bitcast(E5),
-                    lhsT_scale=g_scales[gi][:, 0, P * a : P * (a + 1)],
-                    rhs=wb_codes[:, HALF * h : HALF * (h + 1)].bitcast(E4),
-                    rhs_scale=wb_scales[:, HALF * h : HALF * (h + 1)],
-                    start=True, stop=True,
-                )
+                for rep in range(MX_REPEAT):
+                    nc.tensor.matmul_mx(
+                        out=acc[:],
+                        lhsT=g_codes[gi][:, 0, P * a : P * (a + 1)].bitcast(E5),
+                        lhsT_scale=g_scales[gi][:, 0, P * a : P * (a + 1)],
+                        rhs=wb_codes[:, HALF * h : HALF * (h + 1)].bitcast(E4),
+                        rhs_scale=wb_scales[:, HALF * h : HALF * (h + 1)],
+                        start=True, stop=True,
+                    )
                 nc.vector.scalar_tensor_tensor(
                     out=bs[:, a, :], in0=th[:, a, :], scalar=1.0, in1=acc[:],
                     op0=ALU.add, op1=ALU.mult,
@@ -396,11 +399,12 @@ def tile_efficient_skan_batch_t_kernel(
                 m1_pool(k - LAG_M1)
             if live(k - LAG_B):
                 mx_spline(k - LAG_B)
+            if live(k - LAG_C):
+                finish(k - LAG_C)
+            if live(k - LAG_B):
                 mx_base(k - LAG_B)
             if live(k - LAG_P1):
                 p1_pool(k - LAG_P1)
-            if live(k - LAG_C):
-                finish(k - LAG_C)
             if k == 1:
                 wprep(1)
             if gi < NG and ph in (0, 1):

@@ -105,6 +105,8 @@ def tile_efficient_skan_batch_t_kernel(
 
         quarter = const.tile([P, 1], F32, name="quarter")
         nc.vector.memset(quarter[:], 0.25)
+        half = const.tile([P, 1], F32, name="half")
+        nc.vector.memset(half[:], 0.5)
         warm = const.tile([P, 1], F32, name="warm")
         nc.scalar.activation(out=warm[:], in_=quarter[:], func=ACT.Silu)
         half_pi = const.tile([P, 1], F32, name="half_pi")
@@ -284,9 +286,17 @@ def tile_efficient_skan_batch_t_kernel(
                 out=m_tiles[k // 2][:, 2 * q : 2 * q + 2, :], in_=x_in, func=ACT.Silu,
                 scale=-1.0,
             )
+            if q == 1:
+                nc.scalar.activation(
+                    out=m_tiles[k // 2][:, 2 * q : 2 * q + 2, :],
+                    in_=m_tiles[k // 2][:, 2 * q : 2 * q + 2, :],
+                    func=ACT.Identity, bias=half[:, 0:1], scale=-0.5,
+                )
 
         def m1_pool(k):
             q = k % 2
+            if q == 1:
+                return
             m = m_tiles[k // 2]
             nc.gpsimd.tensor_scalar(
                 out=m[:, 2 * q : 2 * q + 2, :], in0=m[:, 2 * q : 2 * q + 2, :],
@@ -389,10 +399,10 @@ def tile_efficient_skan_batch_t_kernel(
                 cs_act(k - LAG_CS)
             if live(k):
                 r_dve(k)
-            if gi < NG and ph in (1, 2):
-                gt_act(gi, ph - 1)
             if live(k):
                 th_m_act(k)
+            if gi < NG and ph in (1, 2):
+                gt_act(gi, ph - 1)
             if k == 0:
                 wprep(0)
             if live(k - LAG_M1):

@@ -55,15 +55,15 @@ def tile_efficient_skan_batch_t_kernel(
         g_tiles = {}
 
         def load(gi):
-            x_sb = three.tile([P, NA, IN], BF16, tag="x_sb")
-            nc.sync.dma_start(
-                out=x_sb[:],
-                in_=xf[GT * gi : GT * (gi + 1), :].rearrange("(p a) i -> p a i", a=NA),
-            )
             g_sb = two.tile([P, NA, K], BF16, tag="g_sb")
             nc.sync.dma_start(
                 out=g_sb[:],
                 in_=gf[GT * gi : GT * (gi + 1), :].rearrange("(p a) k -> p a k", a=NA),
+            )
+            x_sb = three.tile([P, NA, IN], BF16, tag="x_sb")
+            nc.sync.dma_start(
+                out=x_sb[:],
+                in_=xf[GT * gi : GT * (gi + 1), :].rearrange("(p a) i -> p a i", a=NA),
             )
             x_tiles[gi] = x_sb
             g_tiles[gi] = g_sb
@@ -81,7 +81,6 @@ def tile_efficient_skan_batch_t_kernel(
             in_=coef.rearrange("(b p) o -> b (p o)", p=P),
         )
 
-        load(0)
         w_drams = (wc_dram, base_weight)
         w_raw = []
         for wi in range(2):
@@ -96,7 +95,7 @@ def tile_efficient_skan_batch_t_kernel(
                             256 * u : 256 * (u + 1), HALF * h : HALF * (h + 1)
                         ].rearrange("(p e) i -> p e i", e=2),
                     )
-        load(1)
+            load(h)
 
         ident_bf = const.tile([P, P], BF16, name="ident_bf")
         make_identity(nc, ident_bf[:])
@@ -234,18 +233,15 @@ def tile_efficient_skan_batch_t_kernel(
             xt_tiles[k] = xt
 
         def y_act(k):
-            yq = two.tile([P, 2 * GT], F32, tag="yq")
-            nc.scalar.activation(
-                out=yq[:], in_=xt_tiles[k][:].rearrange("p j t -> p (j t)"),
-                func=ACT.Identity, bias=quarter[:, 0:1], scale=turns[:, 0:1],
-            )
+            yq = two.tile([P, 2 * GT], BF16, tag="yq")
+            nc.scalar.copy(out=yq[:], in_=xt_tiles[k][:].rearrange("p j t -> p (j t)"))
             yq_tiles[k] = yq
 
         def n_pool(k):
             n_i = two.tile([P, 2 * GT], I32, tag="n_i")
             nc.gpsimd.tensor_scalar(
-                out=n_i[:], in0=yq_tiles[k][:], scalar1=1.0, scalar2=0.0,
-                op0=ALU.mult, op1=ALU.add,
+                out=n_i[:], in0=yq_tiles[k][:], scalar1=turns[:, 0:1],
+                scalar2=quarter[:, 0:1], op0=ALU.mult, op1=ALU.add,
             )
             ni_tiles[k] = n_i
 
@@ -286,7 +282,7 @@ def tile_efficient_skan_batch_t_kernel(
                 out=m_tiles[k // 2][:, 2 * q : 2 * q + 2, :], in_=x_in, func=ACT.Silu,
                 scale=-1.0,
             )
-            if q == 1:
+            if k % 4 != 2:
                 nc.scalar.activation(
                     out=m_tiles[k // 2][:, 2 * q : 2 * q + 2, :],
                     in_=m_tiles[k // 2][:, 2 * q : 2 * q + 2, :],
@@ -295,7 +291,7 @@ def tile_efficient_skan_batch_t_kernel(
 
         def m1_pool(k):
             q = k % 2
-            if q == 1:
+            if k % 4 != 2:
                 return
             m = m_tiles[k // 2]
             nc.gpsimd.tensor_scalar(
@@ -379,6 +375,7 @@ def tile_efficient_skan_batch_t_kernel(
         def live(i):
             return 0 <= i < NK
 
+        wprep(0)
         for ap in range(2):
             gt_pe(0, ap)
             gt_act(0, ap)
@@ -404,7 +401,7 @@ def tile_efficient_skan_batch_t_kernel(
             if gi < NG and ph in (1, 2):
                 gt_act(gi, ph - 1)
             if k == 0:
-                wprep(0)
+                wprep(1)
             if live(k - LAG_M1):
                 m1_pool(k - LAG_M1)
             if live(k - LAG_B):
@@ -415,8 +412,6 @@ def tile_efficient_skan_batch_t_kernel(
                 mx_base(k - LAG_B)
             if live(k - LAG_P1):
                 p1_pool(k - LAG_P1)
-            if k == 1:
-                wprep(1)
             if gi < NG and ph in (0, 1):
                 gt_pe(gi, ph)
             if gi < NG and ph == 2:

@@ -299,10 +299,10 @@ def tile_efficient_skan_batch_t_kernel(
                 scalar1=-0.5, scalar2=0.5, op0=ALU.mult, op1=ALU.add,
             )
 
-        def mx_spline(k):
+        def mx_spline(k, j2):
             gi, h, q = split(k)
             sp = sp_tiles[k // 2]
-            for j in (2 * q, 2 * q + 1):
+            for j in (2 * q + j2,):
                 b = 4 * h + j
                 acc = ps.tile([P, GT], F32, tag="mx", bufs=3)
                 for rep in range(MX_REPEAT):
@@ -394,6 +394,8 @@ def tile_efficient_skan_batch_t_kernel(
                 n_pool(k)
             if live(k - LAG_CS):
                 cs_act(k - LAG_CS)
+            if live(k - LAG_B):
+                mx_spline(k - LAG_B, 0)
             if live(k):
                 r_dve(k)
             if live(k):
@@ -405,7 +407,7 @@ def tile_efficient_skan_batch_t_kernel(
             if live(k - LAG_M1):
                 m1_pool(k - LAG_M1)
             if live(k - LAG_B):
-                mx_spline(k - LAG_B)
+                mx_spline(k - LAG_B, 1)
             if live(k - LAG_C):
                 finish(k - LAG_C)
             if live(k - LAG_B):

@@ -241,7 +241,7 @@ def tile_efficient_skan_batch_t_kernel(
             n_i = two.tile([P, 2 * GT], I32, tag="n_i")
             nc.gpsimd.tensor_scalar(
                 out=n_i[:], in0=yq_tiles[k][:], scalar1=turns[:, 0:1],
-                scalar2=quarter[:, 0:1], op0=ALU.mult, op1=ALU.add,
+                scalar2=0.25, op0=ALU.mult, op1=ALU.add,
             )
             ni_tiles[k] = n_i
 
@@ -282,7 +282,7 @@ def tile_efficient_skan_batch_t_kernel(
                 out=m_tiles[k // 2][:, 2 * q : 2 * q + 2, :], in_=x_in, func=ACT.Silu,
                 scale=-1.0,
             )
-            if k % 4 != 2:
+            if k % 4 != 4:
                 nc.scalar.activation(
                     out=m_tiles[k // 2][:, 2 * q : 2 * q + 2, :],
                     in_=m_tiles[k // 2][:, 2 * q : 2 * q + 2, :],
@@ -291,7 +291,7 @@ def tile_efficient_skan_batch_t_kernel(
 
         def m1_pool(k):
             q = k % 2
-            if k % 4 != 2:
+            if k % 4 != 4:
                 return
             m = m_tiles[k // 2]
             nc.gpsimd.tensor_scalar(
@@ -299,10 +299,10 @@ def tile_efficient_skan_batch_t_kernel(
                 scalar1=-0.5, scalar2=0.5, op0=ALU.mult, op1=ALU.add,
             )
 
-        def mx_spline(k, j2):
+        def mx_spline(k):
             gi, h, q = split(k)
             sp = sp_tiles[k // 2]
-            for j in (2 * q + j2,):
+            for j in (2 * q, 2 * q + 1):
                 b = 4 * h + j
                 acc = ps.tile([P, GT], F32, tag="mx", bufs=3)
                 for rep in range(MX_REPEAT):
@@ -394,8 +394,6 @@ def tile_efficient_skan_batch_t_kernel(
                 n_pool(k)
             if live(k - LAG_CS):
                 cs_act(k - LAG_CS)
-            if live(k - LAG_B):
-                mx_spline(k - LAG_B, 0)
             if live(k):
                 r_dve(k)
             if live(k):
@@ -407,7 +405,7 @@ def tile_efficient_skan_batch_t_kernel(
             if live(k - LAG_M1):
                 m1_pool(k - LAG_M1)
             if live(k - LAG_B):
-                mx_spline(k - LAG_B, 1)
+                mx_spline(k - LAG_B)
             if live(k - LAG_C):
                 finish(k - LAG_C)
             if live(k - LAG_B):

import math
from contextlib import ExitStack

import concourse.mybir as mybir
from concourse.masks import make_identity

F32 = mybir.dt.float32
BF16 = mybir.dt.bfloat16
I32 = mybir.dt.int32
U32 = mybir.dt.uint32
U8 = mybir.dt.uint8
E4 = mybir.dt.float8_e4m3fn_x4
E5 = mybir.dt.float8_e5m2_x4
ACT = mybir.ActivationFunctionType
ALU = mybir.AluOpType

P = 128
TOKENS = 4096
K = 512
IN = 1024
GT = 512
NA = GT // P
NG = TOKENS // GT
HALF = 512
NH = IN // HALF
NK = NG * NH * 2

LAG_CS = 1
LAG_B = 1
LAG_M1 = 1
LAG_P1 = 2
LAG_C = 3
MX_REPEAT = 2

FLOPS = 2 * 2 * TOKENS * K * IN


def tile_efficient_skan_batch_t_kernel(
    tc, x, base_weight, grid, scale_sp, coef, conv_w, conv_b, grad_out, out
):
    nc = tc.nc
    xf = x.flatten_outer_dims()
    gf = grad_out.flatten_outer_dims()
    of = out.flatten_outer_dims()
    wc_dram = conv_w.rearrange("o k i -> (o k) i")

    with ExitStack() as ctx:
        const = ctx.enter_context(tc.tile_pool(name="const", bufs=1))
        two = ctx.enter_context(tc.tile_pool(name="two", bufs=2))
        three = ctx.enter_context(tc.tile_pool(name="three", bufs=3))
        ps = ctx.enter_context(tc.psum_pool(name="ps", bufs=2))
        ctx.enter_context(tc.manual_schedule())

        x_tiles = {}
        g_tiles = {}

        def load(gi):
            g_sb = two.tile([P, NA, K], BF16, tag="g_sb")
            nc.sync.dma_start(
                out=g_sb[:],
                in_=gf[GT * gi : GT * (gi + 1), :].rearrange("(p a) k -> p a k", a=NA),
            )
            x_sb = three.tile([P, NA, IN], BF16, tag="x_sb")
            nc.sync.dma_start(
                out=x_sb[:],
                in_=xf[GT * gi : GT * (gi + 1), :].rearrange("(p a) i -> p a i", a=NA),
            )
            x_tiles[gi] = x_sb
            g_tiles[gi] = g_sb

        grid_bf = const.tile([P, 1], BF16, name="grid_bf")
        nc.scalar.dma_start(out=grid_bf[:], in_=grid.partition_broadcast(P))
        sc4 = const.tile([P, 2, 2], BF16, name="sc4")
        nc.scalar.dma_start(
            out=sc4[:], in_=scale_sp.rearrange("(u p e) -> p u e", u=2, e=2)
        )
        coef_rows = const.tile([P, P], BF16, name="coef_rows")
        nc.vector.memset(coef_rows[:], 0.0)
        nc.scalar.dma_start(
            out=coef_rows[0 : IN // P, :],
            in_=coef.rearrange("(b p) o -> b (p o)", p=P),
        )

        w_drams = (wc_dram, base_weight)
        w_raw = []
        for wi in range(2):
            raw = const.tile([P, 4, IN], BF16, name="w_raw%d" % wi)
            w_raw.append(raw)
        for h in range(NH):
            for wi in range(2):
                for u in range(2):
                    nc.sync.dma_start(
                        out=w_raw[wi][:, 2 * u : 2 * u + 2, HALF * h : HALF * (h + 1)],
                        in_=w_drams[wi][
                            256 * u : 256 * (u + 1), HALF * h : HALF * (h + 1)
                        ].rearrange("(p e) i -> p e i", e=2),
                    )
            load(h)

        ident_bf = const.tile([P, P], BF16, name="ident_bf")
        make_identity(nc, ident_bf[:])
        ident_f = const.tile([P, P], F32, name="ident_f")
        make_identity(nc, ident_f[:])

        quarter = const.tile([P, 1], F32, name="quarter")
        nc.vector.memset(quarter[:], 0.25)
        half = const.tile([P, 1], F32, name="half")
        nc.vector.memset(half[:], 0.5)
        warm = const.tile([P, 1], F32, name="warm")
        nc.scalar.activation(out=warm[:], in_=quarter[:], func=ACT.Silu)
        half_pi = const.tile([P, 1], F32, name="half_pi")
        nc.vector.tensor_scalar(
            out=half_pi[:], in0=quarter[:], scalar1=2.0 * math.pi, scalar2=None,
            op0=ALU.mult,
        )
        grid_f = const.tile([P, 1], F32, name="grid_f")
        nc.vector.tensor_copy(out=grid_f[:], in_=grid_bf[:])
        turns = const.tile([P, 1], F32, name="turns")
        nc.vector.tensor_scalar(
            out=turns[:], in0=grid_f[:], scalar1=1.0 / (2.0 * math.pi), scalar2=None,
            op0=ALU.mult,
        )
        coef_ps = ps.tile([P, P], BF16, tag="gt", bufs=1)
        nc.tensor.transpose(out=coef_ps[:], in_=coef_rows[:], identity=ident_bf[:])
        ccol = const.tile([P, IN // P], F32, name="ccol")
        nc.vector.tensor_scalar(
            out=ccol[:], in0=coef_ps[:, 0 : IN // P], scalar1=grid_f[:, 0:1],
            scalar2=None, op0=ALU.mult,
        )

        w_codes = []
        w_scales = []
        for wi in range(2):
            codes = const.tile([P, IN], U32, name="w_codes%d" % wi, align_bytes=64)
            scales = const.tile([P, IN], U8, name="w_scales%d" % wi, align_bytes=64)
            w_codes.append(codes)
            w_scales.append(scales)
        wc_codes, wb_codes = w_codes
        wc_scales, wb_scales = w_scales

        def wprep(h):
            grouped = []
            for wi in range(2):
                grp = two.tile([P, HALF, 4], BF16, tag="grp%d" % wi, align_bytes=64)
                nc.vector.tensor_copy(
                    out=grp[:].rearrange("p (c j) t -> p c t j", j=4),
                    in_=w_raw[wi][:, :, HALF * h : HALF * (h + 1)].rearrange(
                        "p t (c j) -> p c t j", j=4
                    ),
                )
                grouped.append(grp)
            for wi in range(2):
                nc.vector.quantize_mx(
                    out=w_codes[wi][:, HALF * h : HALF * (h + 1)].bitcast(E4),
                    scales=w_scales[wi][:, HALF * h : HALF * (h + 1)],
                    in_=grouped[wi][:].rearrange("p i t -> p (i t)"),
                )

        gt_tiles = {}
        gq_tiles = {}
        g_codes = {}
        g_scales = {}

        def gt_pe(gi, ap):
            g32 = g_tiles[gi][:].bitcast(F32)
            tr = ps.tile([P, 2, 2, P], F32, tag="gt", bufs=1)
            for a2 in range(2):
                for u in range(2):
                    nc.tensor.transpose(
                        out=tr[:, a2, u, :],
                        in_=g32[:, 2 * ap + a2, P * u : P * (u + 1)],
                        identity=ident_f[:],
                    )
            gt_tiles[gi, ap] = tr

        def gt_act(gi, ap):
            if ap == 0:
                gq = two.tile([P, 2, 4 * GT], BF16, tag="gq", align_bytes=64)
                gq_tiles[gi] = gq
            gq = gq_tiles[gi]
            gq32 = gq[:, 0, :].bitcast(F32).rearrange("p (a t u) -> p a t u", a=NA, u=2)
            nc.scalar.copy(
                out=gq32[:, 2 * ap : 2 * ap + 2, :, :],
                in_=gt_tiles[gi, ap][:].rearrange("p a u t -> p a t u"),
            )

        def gs_mul(gi):
            gq = gq_tiles[gi]
            nc.vector.tensor_tensor(
                out=gq[:, 1, :].rearrange("p (t s) -> p t s", s=4),
                in0=gq[:, 0, :].rearrange("p (t s) -> p t s", s=4),
                in1=sc4[:].rearrange("p u e -> p (u e)").unsqueeze(1).to_broadcast([P, GT, 4]),
                op=ALU.mult,
            )

        def quant(gi):
            gq = gq_tiles[gi]
            gc = two.tile([P, 2, GT], U32, tag="gc", align_bytes=64)
            gs = two.tile([P, 2, GT], U8, tag="gs", align_bytes=64)
            nc.vector.quantize_mx(
                out=gc[:].rearrange("p w c -> p (w c)").bitcast(E5),
                scales=gs[:].rearrange("p w c -> p (w c)"),
                in_=gq[:].rearrange("p w c -> p (w c)"),
            )
            g_codes[gi] = gc
            g_scales[gi] = gs

        xt_tiles = {}
        yq_tiles = {}
        ni_tiles = {}
        sp_tiles = {}
        th_tiles = {}
        m_tiles = {}
        bs_tiles = {}

        def split(k):
            gi, rest = divmod(k, 2 * NH)
            h, q = divmod(rest, 2)
            return gi, h, q

        def x_t(k):
            gi, h, q = split(k)
            x_sb = x_tiles[gi]
            xt = ps.tile([P, 2, GT], BF16, tag="tr")
            for j2 in range(2):
                b = 4 * h + 2 * q + j2
                for a in range(NA):
                    nc.tensor.transpose(
                        out=xt[:, j2, P * a : P * (a + 1)],
                        in_=x_sb[:, a, P * b : P * (b + 1)],
                        identity=ident_bf[:],
                    )
            xt_tiles[k] = xt

        def y_act(k):
            yq = two.tile([P, 2 * GT], BF16, tag="yq")
            nc.scalar.copy(out=yq[:], in_=xt_tiles[k][:].rearrange("p j t -> p (j t)"))
            yq_tiles[k] = yq

        def n_pool(k):
            n_i = two.tile([P, 2 * GT], I32, tag="n_i")
            nc.gpsimd.tensor_scalar(
                out=n_i[:], in0=yq_tiles[k][:], scalar1=turns[:, 0:1],
                scalar2=0.25, op0=ALU.mult, op1=ALU.add,
            )
            ni_tiles[k] = n_i

        def r_dve(k):
            q = k % 2
            if q == 0:
                sp = three.tile([P, 4, GT], F32, tag="sp")
                sp_tiles[k // 2] = sp
            sp = sp_tiles[k // 2]
            nc.vector.scalar_tensor_tensor(
                out=sp[:, 2 * q : 2 * q + 2, :].rearrange("p j t -> p (j t)"),
                in0=xt_tiles[k][:].rearrange("p j t -> p (j t)"),
                scalar=turns[:, 0:1], in1=ni_tiles[k][:],
                op0=ALU.mult, op1=ALU.subtract,
            )

        def cs_act(k):
            q = k % 2
            sp = sp_tiles[k // 2]
            nc.scalar.activation(
                out=sp[:, 2 * q : 2 * q + 2, :], in_=sp[:, 2 * q : 2 * q + 2, :],
                func=ACT.Sin, bias=half_pi[:, 0:1], scale=2.0 * math.pi,
            )

        def th_m_act(k):
            gi, h, q = split(k)
            if q == 0:
                th = three.tile([P, NA, HALF], F32, tag="th")
                m = three.tile([P, NA, HALF], F32, tag="m")
                th_tiles[k // 2] = th
                m_tiles[k // 2] = m
            x_in = x_tiles[gi][:, 2 * q : 2 * q + 2, HALF * h : HALF * (h + 1)]
            nc.scalar.activation(
                out=th_tiles[k // 2][:, 2 * q : 2 * q + 2, :], in_=x_in, func=ACT.Tanh,
                scale=0.5,
            )
            nc.scalar.activation(
                out=m_tiles[k // 2][:, 2 * q : 2 * q + 2, :], in_=x_in, func=ACT.Silu,
                scale=-1.0,
            )
            if k % 4 != 4:
                nc.scalar.activation(
                    out=m_tiles[k // 2][:, 2 * q : 2 * q + 2, :],
                    in_=m_tiles[k // 2][:, 2 * q : 2 * q + 2, :],
                    func=ACT.Identity, bias=half[:, 0:1], scale=-0.5,
                )

        def m1_pool(k):
            q = k % 2
            if k % 4 != 4:
                return
            m = m_tiles[k // 2]
            nc.gpsimd.tensor_scalar(
                out=m[:, 2 * q : 2 * q + 2, :], in0=m[:, 2 * q : 2 * q + 2, :],
                scalar1=-0.5, scalar2=0.5, op0=ALU.mult, op1=ALU.add,
            )

        def mx_spline(k):
            gi, h, q = split(k)
            sp = sp_tiles[k // 2]
            for j in (2 * q, 2 * q + 1):
                b = 4 * h + j
                acc = ps.tile([P, GT], F32, tag="mx", bufs=3)
                for rep in range(MX_REPEAT):
                    nc.tensor.matmul_mx(
                        out=acc[:],
                        lhsT=wc_codes[:, P * b : P * (b + 1)].bitcast(E4),
                        lhsT_scale=wc_scales[:, P * b : P * (b + 1)],
                        rhs=g_codes[gi][:, 1, :].bitcast(E5),
                        rhs_scale=g_scales[gi][:, 1, :],
                        start=True, stop=True,
                    )
                nc.vector.scalar_tensor_tensor(
                    out=sp[:, j, :], in0=acc[:], scalar=ccol[:, b : b + 1], in1=sp[:, j, :],
                    op0=ALU.mult, op1=ALU.mult,
                )

        def mx_base(k):
            gi, h, q = split(k)
            if q == 0:
                bs = three.tile([P, NA, HALF], F32, tag="bs")
                bs_tiles[k // 2] = bs
            bs = bs_tiles[k // 2]
            th = th_tiles[k // 2]
            for a in (2 * q, 2 * q + 1):
                acc = ps.tile([P, HALF], F32, tag="mx", bufs=3)
                for rep in range(MX_REPEAT):
                    nc.tensor.matmul_mx(
                        out=acc[:],
                        lhsT=g_codes[gi][:, 0, P * a : P * (a + 1)].bitcast(E5),
                        lhsT_scale=g_scales[gi][:, 0, P * a : P * (a + 1)],
                        rhs=wb_codes[:, HALF * h : HALF * (h + 1)].bitcast(E4),
                        rhs_scale=wb_scales[:, HALF * h : HALF * (h + 1)],
                        start=True, stop=True,
                    )
                nc.vector.scalar_tensor_tensor(
                    out=bs[:, a, :], in0=th[:, a, :], scalar=1.0, in1=acc[:],
                    op0=ALU.add, op1=ALU.mult,
                )

        def p1_pool(k):
            q = k % 2
            bs = bs_tiles[k // 2]
            nc.gpsimd.tensor_tensor(
                out=bs[:, 2 * q : 2 * q + 2, :], in0=bs[:, 2 * q : 2 * q + 2, :],
                in1=m_tiles[k // 2][:, 2 * q : 2 * q + 2, :], op=ALU.mult,
            )

        def finish(k):
            gi, h, q = split(k)
            sp = sp_tiles[k // 2]
            bs = bs_tiles[k // 2]
            for a in (2 * q, 2 * q + 1):
                p2 = ps.tile([P, HALF], F32, tag="p2")
                for j in range(4):
                    nc.tensor.transpose(
                        out=p2[:, P * j : P * (j + 1)],
                        in_=sp[:, j, P * a : P * (a + 1)],
                        identity=ident_f[:],
                    )
                nc.vector.tensor_tensor(
                    out=bs[:, a, :], in0=p2[:], in1=bs[:, a, :], op=ALU.add
                )
            nc.sync.dma_start(
                out=of[GT * gi : GT * (gi + 1), HALF * h : HALF * (h + 1)].rearrange(
                    "(p a) i -> p a i", a=NA
                )[:, 2 * q : 2 * q + 2, :],
                in_=bs[:, 2 * q : 2 * q + 2, :],
            )

        def live(i):
            return 0 <= i < NK

        wprep(0)
        for ap in range(2):
            gt_pe(0, ap)
            gt_act(0, ap)
        gs_mul(0)
        quant(0)
        x_t(0)
        for k in range(NK + LAG_C + 1):
            gi, ph = divmod(k + 4, 4)
            if ph == 0 and gi + 1 < NG:
                load(gi + 1)
            if live(k):
                y_act(k)
            if live(k + 1):
                x_t(k + 1)
            if live(k):
                n_pool(k)
            if live(k - LAG_CS):
                cs_act(k - LAG_CS)
            if live(k):
                r_dve(k)
            if live(k):
                th_m_act(k)
            if gi < NG and ph in (1, 2):
                gt_act(gi, ph - 1)
            if k == 0:
                wprep(1)
            if live(k - LAG_M1):
                m1_pool(k - LAG_M1)
            if live(k - LAG_B):
                mx_spline(k - LAG_B)
            if live(k - LAG_C):
                finish(k - LAG_C)
            if live(k - LAG_B):
                mx_base(k - LAG_B)
            if live(k - LAG_P1):
                p1_pool(k - LAG_P1)
            if gi < NG and ph in (0, 1):
                gt_pe(gi, ph)
            if gi < NG and ph == 2:
                gs_mul(gi)
            if gi < NG and ph == 3:
                quant(gi)
